import numpy as np
import ml_dtypes


def mxq(x, axis, fmt="e4m3"):
    dtype, down = {"e4m3": (ml_dtypes.float8_e4m3fn, 7), "e5m2": (ml_dtypes.float8_e5m2, 14)}[fmt]
    v = np.moveaxis(np.asarray(x, np.float32).astype(ml_dtypes.bfloat16).astype(np.float64), axis, -1)
    blocks = v.reshape(v.shape[:-1] + (-1, 32))
    amax = np.abs(blocks).max(-1, keepdims=True)
    byte = np.maximum(np.where(amax > 0, np.frexp(amax)[1] - 1 + 127, 0) - down, 1)
    scale = np.exp2(byte - 127.0)
    codes = (blocks / scale).astype(np.float32).astype(dtype).astype(np.float64)
    return np.moveaxis((codes * scale).reshape(v.shape), -1, axis)


WIDE = False


def mx_kscale(k):
    if not WIDE:
        return np.ones(k)
    levels = np.array([10, -10, 5, -5, 0])
    a = np.random.permutation(np.resize(levels, k // 512 * 4)).reshape(k // 512, 4)
    idx = np.arange(k)
    return np.exp2(a[idx // 512, idx % 128 // 32])


BF16 = ml_dtypes.bfloat16


def bf(x):
    return np.asarray(x, np.float32).astype(BF16)


def f64(x):
    return np.asarray(x).astype(np.float64)


B, I, H, ORDER = 128, 512, 512, 3
MASK = 1.0 - 0.2


def sigmoid(v):
    return 1.0 / (1.0 + np.exp(-v))


def setup_inputs():
    s = mx_kscale(I)
    return {"x": bf(np.random.standard_normal((B, I)) * s),
            "h": bf(np.random.standard_normal((B, H))),
            "c": bf(np.random.standard_normal((B, H))),
            "mem_read": bf(np.random.standard_normal((B, H)) * 0.55),
            "W_ih": bf(np.random.standard_normal((I, 4 * H)) * 0.7 / np.sqrt(I) / s[:, None]),
            "W_hh": bf(np.random.standard_normal((H, 4 * H)) * 0.7 / np.sqrt(H)),
            "bias": bf(np.random.standard_normal(4 * H) * 0.3)}


def reference(x, h, c, mem_read, W_ih, W_hh, bias):
    h0, c0 = f64(h), f64(c)
    gates = ((mxq(f64(x), 1, "e4m3") @ mxq(f64(W_ih), 0, "e4m3"))
             + (mxq(h0, 1, "e4m3") @ mxq(f64(W_hh), 0, "e4m3"))
             + f64(bias))
    f, i, o, g = np.split(gates, 4, axis=1)
    c_next = sigmoid(f) * c0 + sigmoid(i) * np.tanh(g) + f64(mem_read)
    h_next = sigmoid(o) * np.tanh(c_next)
    h_next = h_next * MASK + h0 * (1.0 - MASK)
    c_next = c_next * MASK + c0 * (1.0 - MASK)
    return h_next, c_next

@@ -1,0 +1,229 @@
+from contextlib import ExitStack
+
+import concourse.mybir as mybir
+from concourse.masks import make_identity
+
+F32 = mybir.dt.float32
+BF16 = mybir.dt.bfloat16
+U32 = mybir.dt.uint32
+U8 = mybir.dt.uint8
+FP8X4 = mybir.dt.float8_e4m3fn_x4
+ACT = mybir.ActivationFunctionType
+ALU = mybir.AluOpType
+
+P = 128
+PACK = 4
+HID = 512
+TILES = HID // P
+GATE_BLOCK = {"f": 0, "i": 1, "o": 2, "g": 3}
+GATE_ORDER = ("i", "g", "f", "o")
+GATE_FUNC = {"f": ACT.Sigmoid, "i": ACT.Sigmoid, "o": ACT.Sigmoid, "g": ACT.Tanh}
+N_UNITS = 2 * len(GATE_ORDER)
+NEW_SHARE = 1.0 - 0.2
+OLD_SHARE = 1.0 - NEW_SHARE
+RUN = 4
+VECTOR_COLS = 224
+
+FLOPS = 2 * P * (2 * HID) * (len(GATE_ORDER) * HID)
+
+
+def gate_closed_by(unit):
+    if 0 <= unit < N_UNITS and unit % 2 == 1:
+        return GATE_ORDER[unit // 2]
+    return None
+
+
+def tile_lstmcell_pb_s_kernel(tc, x, h, c, mem_read, W_ih, W_hh, bias, out_0, out_1):
+    nc = tc.nc
+    units = [(gate, weight) for gate in GATE_ORDER for weight in (W_ih, W_hh)]
+
+    with ExitStack() as ctx:
+        const = ctx.enter_context(tc.tile_pool(name="const", bufs=1))
+        stream = ctx.enter_context(tc.tile_pool(name="stream", bufs=N_UNITS))
+        psum = ctx.enter_context(tc.psum_pool(name="psum", bufs=1))
+
+        warm = const.tile([P, 1], F32)
+        nc.vector.memset(warm[:], 0.0)
+        nc.scalar.activation(out=warm[:], in_=warm[:], func=ACT.Sigmoid)
+        ident_f32 = const.tile([P, P], F32)
+        make_identity(nc, ident_f32[:])
+        ident_bf16 = const.tile([P, P], BF16)
+        make_identity(nc, ident_bf16[:])
+        bias_rows = const.tile([P, P], BF16)
+        nc.vector.memset(bias_rows[:], 0.0)
+
+        nc.scalar.dma_start(
+            out=bias_rows[0 : len(GATE_ORDER) * TILES, :], in_=bias.rearrange("(r q) -> r q", q=P)
+        )
+        x_sb = const.tile([P, HID], BF16)
+        nc.sync.dma_start(out=x_sb[:], in_=x)
+        h_sb = const.tile([P, HID], BF16)
+        nc.sync.dma_start(out=h_sb[:], in_=h)
+        c_sb = const.tile([P, HID], BF16)
+        mem_sb = const.tile([P, HID], BF16)
+        raws = []
+        for unit, (gate, weight) in enumerate(units):
+            first = GATE_BLOCK[gate] * HID
+            raw = stream.tile([P, PACK, HID], BF16)
+            nc.sync.dma_start(
+                out=raw[:], in_=weight[:, first : first + HID].rearrange("(p t) n -> p t n", t=PACK)
+            )
+            raws.append(raw)
+            if unit == 1:
+                nc.sync.dma_start(out=c_sb[:], in_=c)
+                nc.sync.dma_start(out=mem_sb[:], in_=mem_read)
+
+        xh_words = psum.tile([P, 2, 2, P], F32)
+        for s, rows in enumerate((x_sb, h_sb)):
+            words = rows[:].bitcast(F32).rearrange("b (p u) -> b u p", u=2)
+            for u in range(2):
+                nc.tensor.transpose(out=xh_words[:, s, u, :], in_=words[:, u, :], identity=ident_f32[:])
+        xh_grouped = const.tile([P, 2, P, PACK], BF16, align_bytes=64)
+        nc.vector.tensor_copy(
+            out=xh_grouped[:].bitcast(F32), in_=xh_words[:].rearrange("p s u b -> p s b u")
+        )
+        xh_codes = const.tile([P, 2 * P], U32, align_bytes=64)
+        xh_scales = const.tile([P, 2 * P], U8, align_bytes=64)
+
+        bias_ps = psum.tile([P, P], BF16, tag="c_natural")
+        nc.tensor.transpose(out=bias_ps[:], in_=bias_rows[:], identity=ident_bf16[:])
+        bias_col = const.tile([P, len(GATE_ORDER) * TILES], F32)
+        nc.vector.tensor_copy(out=bias_col[:], in_=bias_ps[:, 0 : len(GATE_ORDER) * TILES])
+        cm_T = psum.tile([P, 2, TILES, P], BF16)
+        for s, rows in enumerate((c_sb, mem_sb)):
+            for m in range(TILES):
+                nc.tensor.transpose(
+                    out=cm_T[:, s, m, :], in_=rows[:, m * P : (m + 1) * P], identity=ident_bf16[:]
+                )
+
+        groupeds = []
+        codes = []
+        scales = []
+        gate_ps = {}
+        gate_act = {}
+
+        def regroup(unit):
+            grouped = stream.tile([P, HID, PACK], BF16, align_bytes=64)
+            groupeds.append(grouped)
+            for copy, cols in (
+                (nc.vector.tensor_copy, slice(0, VECTOR_COLS)),
+                (nc.scalar.copy, slice(VECTOR_COLS, HID)),
+            ):
+                copy(
+                    out=grouped[:, cols, :].rearrange("p (n i) t -> p n t i", i=RUN),
+                    in_=raws[unit][:, :, cols].rearrange("p t (n i) -> p n t i", i=RUN),
+                )
+
+        def quantise(unit):
+            code = stream.tile([P, HID], U32, align_bytes=64)
+            scale = stream.tile([P, HID], U8, align_bytes=64)
+            nc.vector.quantize_mx(
+                out=code[:].bitcast(FP8X4),
+                scales=scale[:],
+                in_=groupeds[unit][:].rearrange("p n t -> p (n t)"),
+            )
+            codes.append(code)
+            scales.append(scale)
+
+        def passes(gate):
+            last = 2 * GATE_ORDER.index(gate) + 1
+            bank = psum.tile([P, TILES, P], F32, name="bank_%s" % gate)
+            gate_ps[gate] = bank
+            for m in range(TILES):
+                cols = slice(m * P, (m + 1) * P)
+                for s, unit in enumerate((last - 1, last)):
+                    nc.tensor.matmul_mx(
+                        out=bank[:, m, :],
+                        lhsT=codes[unit][:, cols].bitcast(FP8X4),
+                        lhsT_scale=scales[unit][:, cols],
+                        rhs=xh_codes[:, s * P : (s + 1) * P].bitcast(FP8X4),
+                        rhs_scale=xh_scales[:, s * P : (s + 1) * P],
+                        start=(s == 0),
+                        stop=(s == 1),
+                    )
+
+        def activations(gate):
+            act = const.tile([P, TILES, P], F32, name="act_%s" % gate)
+            gate_act[gate] = act
+            for m in range(TILES):
+                r = GATE_BLOCK[gate] * TILES + m
+                nc.scalar.activation(
+                    out=act[:, m, :],
+                    in_=gate_ps[gate][:, m, :],
+                    func=GATE_FUNC[gate],
+                    bias=bias_col[:, r : r + 1],
+                )
+
+        fresh8 = const.tile([P, TILES, P], F32)
+        added8 = const.tile([P, TILES, P], F32)
+        kept8 = const.tile([P, TILES, P], F32)
+        cn8 = const.tile([P, TILES, P], F32)
+        tanh_cn = const.tile([P, TILES, P], F32)
+        hn8 = const.tile([P, TILES, P], F32)
+        natural = {}
+
+        def to_natural(gate, state8, tag):
+            back = psum.tile([P, HID], F32, name="natural_%s" % gate, tag=tag)
+            natural[gate] = back
+            for m in range(TILES):
+                nc.tensor.transpose(
+                    out=back[:, m * P : (m + 1) * P], in_=state8[:, m, :], identity=ident_f32[:]
+                )
+
+        def elementwise(gate):
+            if gate == "g":
+                nc.vector.scalar_tensor_tensor(
+                    out=fresh8[:], in0=gate_act["i"][:], scalar=NEW_SHARE, in1=gate_act["g"][:],
+                    op0=ALU.mult, op1=ALU.mult,
+                )
+                nc.vector.scalar_tensor_tensor(
+                    out=added8[:], in0=cm_T[:, 1], scalar=NEW_SHARE, in1=fresh8[:],
+                    op0=ALU.mult, op1=ALU.add,
+                )
+            if gate == "f":
+                nc.vector.scalar_tensor_tensor(
+                    out=kept8[:], in0=gate_act["f"][:], scalar=NEW_SHARE, in1=cm_T[:, 0],
+                    op0=ALU.mult, op1=ALU.mult,
+                )
+                nc.vector.tensor_tensor(out=cn8[:], in0=kept8[:], in1=added8[:], op=ALU.add)
+                nc.scalar.activation(out=tanh_cn[:], in_=cn8[:], func=ACT.Tanh, scale=1.0 / NEW_SHARE)
+                to_natural("f", cn8, "c_natural")
+            if gate == "o":
+                nc.vector.scalar_tensor_tensor(
+                    out=hn8[:], in0=gate_act["o"][:], scalar=NEW_SHARE, in1=tanh_cn[:],
+                    op0=ALU.mult, op1=ALU.mult,
+                )
+                to_natural("o", hn8, "h_natural")
+
+        def blend(gate):
+            if gate in ("f", "o"):
+                old, out = {"f": (c_sb, out_1), "o": (h_sb, out_0)}[gate]
+                result = const.tile([P, HID], F32, name="result_%s" % gate)
+                nc.vector.scalar_tensor_tensor(
+                    out=result[:], in0=old[:], scalar=OLD_SHARE, in1=natural[gate][:],
+                    op0=ALU.mult, op1=ALU.add,
+                )
+                nc.sync.dma_start(out=out, in_=result[:])
+
+        for step in range(N_UNITS + 3):
+            activations_of = gate_closed_by(step - 2)
+            if activations_of is not None:
+                activations(activations_of)
+            if step < N_UNITS:
+                regroup(step)
+            if step == 0:
+                nc.vector.quantize_mx(
+                    out=xh_codes[:].bitcast(FP8X4),
+                    scales=xh_scales[:],
+                    in_=xh_grouped[:].rearrange("p s b t -> p (s b t)"),
+                )
+            if 1 <= step <= N_UNITS:
+                quantise(step - 1)
+            passes_of = gate_closed_by(step - 1)
+            if passes_of is not None:
+                passes(passes_of)
+            if activations_of is not None:
+                elementwise(activations_of)
+            blend_of = gate_closed_by(step - 3)
+            if blend_of is not None:
+                blend(blend_of)

@@ -22,7 +22,8 @@ N_UNITS = 2 * len(GATE_ORDER)
 NEW_SHARE = 1.0 - 0.2
 OLD_SHARE = 1.0 - NEW_SHARE
 RUN = 4
-VECTOR_COLS = 224
+VECTOR_COLS = 256
+ACT_LAG = 4
 
 FLOPS = 2 * P * (2 * HID) * (len(GATE_ORDER) * HID)
 
@@ -35,12 +36,12 @@ def gate_closed_by(unit):
 
 def tile_lstmcell_pb_s_kernel(tc, x, h, c, mem_read, W_ih, W_hh, bias, out_0, out_1):
     nc = tc.nc
-    units = [(gate, weight) for gate in GATE_ORDER for weight in (W_ih, W_hh)]
+    units = [(gate, s) for gate in GATE_ORDER for s in range(2)]
 
     with ExitStack() as ctx:
         const = ctx.enter_context(tc.tile_pool(name="const", bufs=1))
-        stream = ctx.enter_context(tc.tile_pool(name="stream", bufs=N_UNITS))
         psum = ctx.enter_context(tc.psum_pool(name="psum", bufs=1))
+        ctx.enter_context(tc.manual_schedule())
 
         warm = const.tile([P, 1], F32)
         nc.vector.memset(warm[:], 0.0)
@@ -61,15 +62,22 @@ def tile_lstmcell_pb_s_kernel(tc, x, h, c, mem_read, W_ih, W_hh, bias, out_0, ou
         nc.sync.dma_start(out=h_sb[:], in_=h)
         c_sb = const.tile([P, HID], BF16)
         mem_sb = const.tile([P, HID], BF16)
-        raws = []
-        for unit, (gate, weight) in enumerate(units):
-            first = GATE_BLOCK[gate] * HID
-            raw = stream.tile([P, PACK, HID], BF16)
+        raw = {}
+        grouped = {}
+        codes = {}
+        scales = {}
+        for key in units:
+            gate, s = key
+            raw[key] = const.tile([P, PACK, HID], BF16, name="raw_%s%d" % key)
+            grouped[key] = const.tile([P, HID, PACK], BF16, name="grouped_%s%d" % key, align_bytes=64)
+            codes[key] = const.tile([P, HID], U32, name="codes_%s%d" % key, align_bytes=64)
+            scales[key] = const.tile([P, HID], U8, name="scales_%s%d" % key, align_bytes=64)
+            block = GATE_BLOCK[gate] * HID
             nc.sync.dma_start(
-                out=raw[:], in_=weight[:, first : first + HID].rearrange("(p t) n -> p t n", t=PACK)
+                out=raw[key][:],
+                in_=(W_ih, W_hh)[s][:, block : block + HID].rearrange("(p t) n -> p t n", t=PACK),
             )
-            raws.append(raw)
-            if unit == 1:
+            if key == units[1]:
                 nc.sync.dma_start(out=c_sb[:], in_=c)
                 nc.sync.dma_start(out=mem_sb[:], in_=mem_read)
 
@@ -79,16 +87,14 @@ def tile_lstmcell_pb_s_kernel(tc, x, h, c, mem_read, W_ih, W_hh, bias, out_0, ou
             for u in range(2):
                 nc.tensor.transpose(out=xh_words[:, s, u, :], in_=words[:, u, :], identity=ident_f32[:])
         xh_grouped = const.tile([P, 2, P, PACK], BF16, align_bytes=64)
-        nc.vector.tensor_copy(
-            out=xh_grouped[:].bitcast(F32), in_=xh_words[:].rearrange("p s u b -> p s b u")
-        )
+        nc.scalar.copy(out=xh_grouped[:].bitcast(F32), in_=xh_words[:].rearrange("p s u b -> p s b u"))
         xh_codes = const.tile([P, 2 * P], U32, align_bytes=64)
         xh_scales = const.tile([P, 2 * P], U8, align_bytes=64)
 
         bias_ps = psum.tile([P, P], BF16, tag="c_natural")
         nc.tensor.transpose(out=bias_ps[:], in_=bias_rows[:], identity=ident_bf16[:])
         bias_col = const.tile([P, len(GATE_ORDER) * TILES], F32)
-        nc.vector.tensor_copy(out=bias_col[:], in_=bias_ps[:, 0 : len(GATE_ORDER) * TILES])
+        nc.scalar.copy(out=bias_col[:], in_=bias_ps[:, 0 : len(GATE_ORDER) * TILES])
         cm_T = psum.tile([P, 2, TILES, P], BF16)
         for s, rows in enumerate((c_sb, mem_sb)):
             for m in range(TILES):
@@ -96,46 +102,37 @@ def tile_lstmcell_pb_s_kernel(tc, x, h, c, mem_read, W_ih, W_hh, bias, out_0, ou
                     out=cm_T[:, s, m, :], in_=rows[:, m * P : (m + 1) * P], identity=ident_bf16[:]
                 )
 
-        groupeds = []
-        codes = []
-        scales = []
         gate_ps = {}
         gate_act = {}
+        for gate in GATE_ORDER:
+            gate_ps[gate] = psum.tile([P, TILES, P], F32, name="bank_%s" % gate)
+            gate_act[gate] = const.tile([P, TILES, P], F32, name="act_%s" % gate)
 
-        def regroup(unit):
-            grouped = stream.tile([P, HID, PACK], BF16, align_bytes=64)
-            groupeds.append(grouped)
+        def regroup(key):
             for copy, cols in (
                 (nc.vector.tensor_copy, slice(0, VECTOR_COLS)),
                 (nc.scalar.copy, slice(VECTOR_COLS, HID)),
             ):
                 copy(
-                    out=grouped[:, cols, :].rearrange("p (n i) t -> p n t i", i=RUN),
-                    in_=raws[unit][:, :, cols].rearrange("p t (n i) -> p n t i", i=RUN),
+                    out=grouped[key][:, cols, :].rearrange("p (n i) t -> p n t i", i=RUN),
+                    in_=raw[key][:, :, cols].rearrange("p t (n i) -> p n t i", i=RUN),
                 )
 
-        def quantise(unit):
-            code = stream.tile([P, HID], U32, align_bytes=64)
-            scale = stream.tile([P, HID], U8, align_bytes=64)
+        def quantise(key):
             nc.vector.quantize_mx(
-                out=code[:].bitcast(FP8X4),
-                scales=scale[:],
-                in_=groupeds[unit][:].rearrange("p n t -> p (n t)"),
+                out=codes[key][:].bitcast(FP8X4),
+                scales=scales[key][:],
+                in_=grouped[key][:].rearrange("p n t -> p (n t)"),
             )
-            codes.append(code)
-            scales.append(scale)
 
         def passes(gate):
-            last = 2 * GATE_ORDER.index(gate) + 1
-            bank = psum.tile([P, TILES, P], F32, name="bank_%s" % gate)
-            gate_ps[gate] = bank
             for m in range(TILES):
                 cols = slice(m * P, (m + 1) * P)
-                for s, unit in enumerate((last - 1, last)):
+                for s in range(2):
                     nc.tensor.matmul_mx(
-                        out=bank[:, m, :],
-                        lhsT=codes[unit][:, cols].bitcast(FP8X4),
-                        lhsT_scale=scales[unit][:, cols],
+                        out=gate_ps[gate][:, m, :],
+                        lhsT=codes[gate, s][:, cols].bitcast(FP8X4),
+                        lhsT_scale=scales[gate, s][:, cols],
                         rhs=xh_codes[:, s * P : (s + 1) * P].bitcast(FP8X4),
                         rhs_scale=xh_scales[:, s * P : (s + 1) * P],
                         start=(s == 0),
@@ -143,74 +140,18 @@ def tile_lstmcell_pb_s_kernel(tc, x, h, c, mem_read, W_ih, W_hh, bias, out_0, ou
                     )
 
         def activations(gate):
-            act = const.tile([P, TILES, P], F32, name="act_%s" % gate)
-            gate_act[gate] = act
             for m in range(TILES):
                 r = GATE_BLOCK[gate] * TILES + m
                 nc.scalar.activation(
-                    out=act[:, m, :],
+                    out=gate_act[gate][:, m, :],
                     in_=gate_ps[gate][:, m, :],
                     func=GATE_FUNC[gate],
                     bias=bias_col[:, r : r + 1],
                 )
 
-        fresh8 = const.tile([P, TILES, P], F32)
-        added8 = const.tile([P, TILES, P], F32)
-        kept8 = const.tile([P, TILES, P], F32)
-        cn8 = const.tile([P, TILES, P], F32)
-        tanh_cn = const.tile([P, TILES, P], F32)
-        hn8 = const.tile([P, TILES, P], F32)
-        natural = {}
-
-        def to_natural(gate, state8, tag):
-            back = psum.tile([P, HID], F32, name="natural_%s" % gate, tag=tag)
-            natural[gate] = back
-            for m in range(TILES):
-                nc.tensor.transpose(
-                    out=back[:, m * P : (m + 1) * P], in_=state8[:, m, :], identity=ident_f32[:]
-                )
-
-        def elementwise(gate):
-            if gate == "g":
-                nc.vector.scalar_tensor_tensor(
-                    out=fresh8[:], in0=gate_act["i"][:], scalar=NEW_SHARE, in1=gate_act["g"][:],
-                    op0=ALU.mult, op1=ALU.mult,
-                )
-                nc.vector.scalar_tensor_tensor(
-                    out=added8[:], in0=cm_T[:, 1], scalar=NEW_SHARE, in1=fresh8[:],
-                    op0=ALU.mult, op1=ALU.add,
-                )
-            if gate == "f":
-                nc.vector.scalar_tensor_tensor(
-                    out=kept8[:], in0=gate_act["f"][:], scalar=NEW_SHARE, in1=cm_T[:, 0],
-                    op0=ALU.mult, op1=ALU.mult,
-                )
-                nc.vector.tensor_tensor(out=cn8[:], in0=kept8[:], in1=added8[:], op=ALU.add)
-                nc.scalar.activation(out=tanh_cn[:], in_=cn8[:], func=ACT.Tanh, scale=1.0 / NEW_SHARE)
-                to_natural("f", cn8, "c_natural")
-            if gate == "o":
-                nc.vector.scalar_tensor_tensor(
-                    out=hn8[:], in0=gate_act["o"][:], scalar=NEW_SHARE, in1=tanh_cn[:],
-                    op0=ALU.mult, op1=ALU.mult,
-                )
-                to_natural("o", hn8, "h_natural")
-
-        def blend(gate):
-            if gate in ("f", "o"):
-                old, out = {"f": (c_sb, out_1), "o": (h_sb, out_0)}[gate]
-                result = const.tile([P, HID], F32, name="result_%s" % gate)
-                nc.vector.scalar_tensor_tensor(
-                    out=result[:], in0=old[:], scalar=OLD_SHARE, in1=natural[gate][:],
-                    op0=ALU.mult, op1=ALU.add,
-                )
-                nc.sync.dma_start(out=out, in_=result[:])
-
-        for step in range(N_UNITS + 3):
-            activations_of = gate_closed_by(step - 2)
-            if activations_of is not None:
-                activations(activations_of)
+        for step in range(N_UNITS + ACT_LAG + 1):
             if step < N_UNITS:
-                regroup(step)
+                regroup(units[step])
             if step == 0:
                 nc.vector.quantize_mx(
                     out=xh_codes[:].bitcast(FP8X4),
@@ -218,12 +159,51 @@ def tile_lstmcell_pb_s_kernel(tc, x, h, c, mem_read, W_ih, W_hh, bias, out_0, ou
                     in_=xh_grouped[:].rearrange("p s b t -> p (s b t)"),
                 )
             if 1 <= step <= N_UNITS:
-                quantise(step - 1)
-            passes_of = gate_closed_by(step - 1)
-            if passes_of is not None:
-                passes(passes_of)
-            if activations_of is not None:
-                elementwise(activations_of)
-            blend_of = gate_closed_by(step - 3)
-            if blend_of is not None:
-                blend(blend_of)
+                quantise(units[step - 1])
+            if gate_closed_by(step - 1) is not None:
+                passes(gate_closed_by(step - 1))
+            if gate_closed_by(step - ACT_LAG) is not None:
+                activations(gate_closed_by(step - ACT_LAG))
+
+        fresh8 = const.tile([P, TILES, P], F32)
+        added8 = const.tile([P, TILES, P], F32)
+        kept8 = const.tile([P, TILES, P], F32)
+        cn8 = const.tile([P, TILES, P], F32)
+        tanh_cn = const.tile([P, TILES, P], F32)
+        hn8 = const.tile([P, TILES, P], F32)
+        c_natural = psum.tile([P, HID], F32, tag="c_natural")
+        h_natural = psum.tile([P, HID], F32)
+        nc.vector.scalar_tensor_tensor(
+            out=fresh8[:], in0=gate_act["i"][:], scalar=NEW_SHARE, in1=gate_act["g"][:],
+            op0=ALU.mult, op1=ALU.mult,
+        )
+        nc.vector.scalar_tensor_tensor(
+            out=added8[:], in0=cm_T[:, 1], scalar=NEW_SHARE, in1=fresh8[:], op0=ALU.mult, op1=ALU.add
+        )
+        for m in range(TILES):
+            nc.vector.scalar_tensor_tensor(
+                out=kept8[:, m, :], in0=gate_act["f"][:, m, :], scalar=NEW_SHARE, in1=cm_T[:, 0, m, :],
+                op0=ALU.mult, op1=ALU.mult,
+            )
+            nc.vector.tensor_tensor(out=cn8[:, m, :], in0=kept8[:, m, :], in1=added8[:, m, :], op=ALU.add)
+            nc.scalar.activation(
+                out=tanh_cn[:, m, :], in_=cn8[:, m, :], func=ACT.Tanh, scale=1.0 / NEW_SHARE
+            )
+            nc.tensor.transpose(
+                out=c_natural[:, m * P : (m + 1) * P], in_=cn8[:, m, :], identity=ident_f32[:]
+            )
+        for m in range(TILES):
+            nc.vector.scalar_tensor_tensor(
+                out=hn8[:, m, :], in0=gate_act["o"][:, m, :], scalar=NEW_SHARE, in1=tanh_cn[:, m, :],
+                op0=ALU.mult, op1=ALU.mult,
+            )
+            nc.tensor.transpose(
+                out=h_natural[:, m * P : (m + 1) * P], in_=hn8[:, m, :], identity=ident_f32[:]
+            )
+
+        for old, new8, out in ((c_sb, c_natural, out_1), (h_sb, h_natural, out_0)):
+            result = const.tile([P, HID], F32, bufs=2)
+            nc.vector.scalar_tensor_tensor(
+                out=result[:], in0=old[:], scalar=OLD_SHARE, in1=new8[:], op0=ALU.mult, op1=ALU.add
+            )
+            nc.sync.dma_start(out=out, in_=result[:])

@@ -57,9 +57,7 @@ def tile_lstmcell_pb_s_kernel(tc, x, h, c, mem_read, W_ih, W_hh, bias, out_0, ou
             out=bias_rows[0 : len(GATE_ORDER) * TILES, :], in_=bias.rearrange("(r q) -> r q", q=P)
         )
         x_sb = const.tile([P, HID], BF16)
-        nc.sync.dma_start(out=x_sb[:], in_=x)
         h_sb = const.tile([P, HID], BF16)
-        nc.sync.dma_start(out=h_sb[:], in_=h)
         c_sb = const.tile([P, HID], BF16)
         mem_sb = const.tile([P, HID], BF16)
         raw = {}
@@ -77,30 +75,12 @@ def tile_lstmcell_pb_s_kernel(tc, x, h, c, mem_read, W_ih, W_hh, bias, out_0, ou
                 out=raw[key][:],
                 in_=(W_ih, W_hh)[s][:, block : block + HID].rearrange("(p t) n -> p t n", t=PACK),
             )
-            if key == units[1]:
-                nc.sync.dma_start(out=c_sb[:], in_=c)
+            if key == units[0]:
+                nc.sync.dma_start(out=x_sb[:], in_=x)
+                nc.sync.dma_start(out=h_sb[:], in_=h)
+            if key == ("g", 1):
                 nc.sync.dma_start(out=mem_sb[:], in_=mem_read)
-
-        xh_words = psum.tile([P, 2, 2, P], F32)
-        for s, rows in enumerate((x_sb, h_sb)):
-            words = rows[:].bitcast(F32).rearrange("b (p u) -> b u p", u=2)
-            for u in range(2):
-                nc.tensor.transpose(out=xh_words[:, s, u, :], in_=words[:, u, :], identity=ident_f32[:])
-        xh_grouped = const.tile([P, 2, P, PACK], BF16, align_bytes=64)
-        nc.scalar.copy(out=xh_grouped[:].bitcast(F32), in_=xh_words[:].rearrange("p s u b -> p s b u"))
-        xh_codes = const.tile([P, 2 * P], U32, align_bytes=64)
-        xh_scales = const.tile([P, 2 * P], U8, align_bytes=64)
-
-        bias_ps = psum.tile([P, P], BF16, tag="c_natural")
-        nc.tensor.transpose(out=bias_ps[:], in_=bias_rows[:], identity=ident_bf16[:])
-        bias_col = const.tile([P, len(GATE_ORDER) * TILES], F32)
-        nc.scalar.copy(out=bias_col[:], in_=bias_ps[:, 0 : len(GATE_ORDER) * TILES])
-        cm_T = psum.tile([P, 2, TILES, P], BF16)
-        for s, rows in enumerate((c_sb, mem_sb)):
-            for m in range(TILES):
-                nc.tensor.transpose(
-                    out=cm_T[:, s, m, :], in_=rows[:, m * P : (m + 1) * P], identity=ident_bf16[:]
-                )
+        nc.sync.dma_start(out=c_sb[:], in_=c)
 
         gate_ps = {}
         gate_act = {}
@@ -149,17 +129,45 @@ def tile_lstmcell_pb_s_kernel(tc, x, h, c, mem_read, W_ih, W_hh, bias, out_0, ou
                     bias=bias_col[:, r : r + 1],
                 )
 
-        for step in range(N_UNITS + ACT_LAG + 1):
+        regroup(units[0])
+
+        xh_words = psum.tile([P, 2, 2, P], F32)
+        for s, rows in enumerate((x_sb, h_sb)):
+            words = rows[:].bitcast(F32).rearrange("b (p u) -> b u p", u=2)
+            for u in range(2):
+                nc.tensor.transpose(out=xh_words[:, s, u, :], in_=words[:, u, :], identity=ident_f32[:])
+        xh_grouped = const.tile([P, 2, P, PACK], BF16, align_bytes=64)
+        nc.scalar.copy(out=xh_grouped[:].bitcast(F32), in_=xh_words[:].rearrange("p s u b -> p s b u"))
+        xh_codes = const.tile([P, 2 * P], U32, align_bytes=64)
+        xh_scales = const.tile([P, 2 * P], U8, align_bytes=64)
+
+        bias_ps = psum.tile([P, P], BF16, tag="c_natural")
+        nc.tensor.transpose(out=bias_ps[:], in_=bias_rows[:], identity=ident_bf16[:])
+        bias_col = const.tile([P, len(GATE_ORDER) * TILES], F32)
+        nc.scalar.copy(out=bias_col[:], in_=bias_ps[:, 0 : len(GATE_ORDER) * TILES])
+        cm_T = psum.tile([P, 2, TILES, P], BF16)
+
+        def to_hidden_major(which, rows):
+            for m in range(TILES):
+                nc.tensor.transpose(
+                    out=cm_T[:, which, m, :], in_=rows[:, m * P : (m + 1) * P], identity=ident_bf16[:]
+                )
+
+        for step in range(1, N_UNITS + ACT_LAG + 1):
             if step < N_UNITS:
                 regroup(units[step])
-            if step == 0:
+            if step <= N_UNITS:
+                quantise(units[step - 1])
+                if units[step - 1] == ("g", 1):
+                    to_hidden_major(1, mem_sb)
+                if units[step - 1] == ("o", 1):
+                    to_hidden_major(0, c_sb)
+            if step == 1:
                 nc.vector.quantize_mx(
                     out=xh_codes[:].bitcast(FP8X4),
                     scales=xh_scales[:],
                     in_=xh_grouped[:].rearrange("p s b t -> p (s b t)"),
                 )
-            if 1 <= step <= N_UNITS:
-                quantise(units[step - 1])
             if gate_closed_by(step - 1) is not None:
                 passes(gate_closed_by(step - 1))
             if gate_closed_by(step - ACT_LAG) is not None:

@@ -18,20 +18,12 @@ TILES = HID // P
 GATE_BLOCK = {"f": 0, "i": 1, "o": 2, "g": 3}
 GATE_ORDER = ("i", "g", "f", "o")
 GATE_FUNC = {"f": ACT.Sigmoid, "i": ACT.Sigmoid, "o": ACT.Sigmoid, "g": ACT.Tanh}
-N_UNITS = 2 * len(GATE_ORDER)
 NEW_SHARE = 1.0 - 0.2
 OLD_SHARE = 1.0 - NEW_SHARE
 RUN = 4
-VECTOR_COLS = 256
-ACT_LAG = 4
+VECTOR_COLS = 272
 
 FLOPS = 2 * P * (2 * HID) * (len(GATE_ORDER) * HID)
-
-
-def gate_closed_by(unit):
-    if 0 <= unit < N_UNITS and unit % 2 == 1:
-        return GATE_ORDER[unit // 2]
-    return None
 
 
 def tile_lstmcell_pb_s_kernel(tc, x, h, c, mem_read, W_ih, W_hh, bias, out_0, out_1):
@@ -75,12 +67,13 @@ def tile_lstmcell_pb_s_kernel(tc, x, h, c, mem_read, W_ih, W_hh, bias, out_0, ou
                 out=raw[key][:],
                 in_=(W_ih, W_hh)[s][:, block : block + HID].rearrange("(p t) n -> p t n", t=PACK),
             )
-            if key == units[0]:
+            if key == units[1]:
                 nc.sync.dma_start(out=x_sb[:], in_=x)
                 nc.sync.dma_start(out=h_sb[:], in_=h)
             if key == ("g", 1):
                 nc.sync.dma_start(out=mem_sb[:], in_=mem_read)
-        nc.sync.dma_start(out=c_sb[:], in_=c)
+            if key == ("f", 1):
+                nc.sync.dma_start(out=c_sb[:], in_=c)
 
         gate_ps = {}
         gate_act = {}
@@ -119,8 +112,8 @@ def tile_lstmcell_pb_s_kernel(tc, x, h, c, mem_read, W_ih, W_hh, bias, out_0, ou
                         stop=(s == 1),
                     )
 
-        def activations(gate):
-            for m in range(TILES):
+        def activations(gate, tiles=range(TILES)):
+            for m in tiles:
                 r = GATE_BLOCK[gate] * TILES + m
                 nc.scalar.activation(
                     out=gate_act[gate][:, m, :],
@@ -129,7 +122,9 @@ def tile_lstmcell_pb_s_kernel(tc, x, h, c, mem_read, W_ih, W_hh, bias, out_0, ou
                     bias=bias_col[:, r : r + 1],
                 )
 
-        regroup(units[0])
+        regroup(("i", 0))
+        quantise(("i", 0))
+        regroup(("i", 1))
 
         xh_words = psum.tile([P, 2, 2, P], F32)
         for s, rows in enumerate((x_sb, h_sb)):
@@ -153,65 +148,85 @@ def tile_lstmcell_pb_s_kernel(tc, x, h, c, mem_read, W_ih, W_hh, bias, out_0, ou
                     out=cm_T[:, which, m, :], in_=rows[:, m * P : (m + 1) * P], identity=ident_bf16[:]
                 )
 
-        for step in range(1, N_UNITS + ACT_LAG + 1):
-            if step < N_UNITS:
-                regroup(units[step])
-            if step <= N_UNITS:
-                quantise(units[step - 1])
-                if units[step - 1] == ("g", 1):
-                    to_hidden_major(1, mem_sb)
-                if units[step - 1] == ("o", 1):
-                    to_hidden_major(0, c_sb)
-            if step == 1:
-                nc.vector.quantize_mx(
-                    out=xh_codes[:].bitcast(FP8X4),
-                    scales=xh_scales[:],
-                    in_=xh_grouped[:].rearrange("p s b t -> p (s b t)"),
-                )
-            if gate_closed_by(step - 1) is not None:
-                passes(gate_closed_by(step - 1))
-            if gate_closed_by(step - ACT_LAG) is not None:
-                activations(gate_closed_by(step - ACT_LAG))
-
         fresh8 = const.tile([P, TILES, P], F32)
         added8 = const.tile([P, TILES, P], F32)
         kept8 = const.tile([P, TILES, P], F32)
         cn8 = const.tile([P, TILES, P], F32)
         tanh_cn = const.tile([P, TILES, P], F32)
         hn8 = const.tile([P, TILES, P], F32)
+
         c_natural = psum.tile([P, HID], F32, tag="c_natural")
         h_natural = psum.tile([P, HID], F32)
+
+        def to_batch_major(natural, rows, half):
+            for m in range(half.start, half.stop):
+                nc.tensor.transpose(
+                    out=natural[:, m * P : (m + 1) * P], in_=rows[:, m, :], identity=ident_f32[:]
+                )
+
+        def blend(old, new8, out, cols):
+            result = const.tile([P, cols.stop - cols.start], F32, name="result", bufs=3)
+            nc.vector.scalar_tensor_tensor(
+                out=result[:], in0=old[:, cols], scalar=OLD_SHARE, in1=new8[:, cols], op0=ALU.mult, op1=ALU.add
+            )
+            nc.sync.dma_start(out=out[:, cols], in_=result[:])
+
+        regroup(("g", 0))
+        quantise(("i", 1))
+        nc.vector.quantize_mx(
+            out=xh_codes[:].bitcast(FP8X4),
+            scales=xh_scales[:],
+            in_=xh_grouped[:].rearrange("p s b t -> p (s b t)"),
+        )
+        passes("i")
+        regroup(("g", 1))
+        quantise(("g", 0))
+        activations("i")
+        regroup(("f", 0))
+        quantise(("g", 1))
+        passes("g")
+        to_hidden_major(1, mem_sb)
+        regroup(("f", 1))
+        quantise(("f", 0))
+        activations("g")
+        regroup(("o", 0))
+        quantise(("f", 1))
+        passes("f")
+        to_hidden_major(0, c_sb)
+        regroup(("o", 1))
+        activations("f")
         nc.vector.scalar_tensor_tensor(
             out=fresh8[:], in0=gate_act["i"][:], scalar=NEW_SHARE, in1=gate_act["g"][:],
             op0=ALU.mult, op1=ALU.mult,
         )
+        quantise(("o", 0))
         nc.vector.scalar_tensor_tensor(
             out=added8[:], in0=cm_T[:, 1], scalar=NEW_SHARE, in1=fresh8[:], op0=ALU.mult, op1=ALU.add
         )
-        for m in range(TILES):
+        halves = [slice(0, TILES // 2), slice(TILES // 2, TILES)]
+        for half in halves:
             nc.vector.scalar_tensor_tensor(
-                out=kept8[:, m, :], in0=gate_act["f"][:, m, :], scalar=NEW_SHARE, in1=cm_T[:, 0, m, :],
+                out=kept8[:, half, :], in0=gate_act["f"][:, half, :], scalar=NEW_SHARE, in1=cm_T[:, 0, half, :],
                 op0=ALU.mult, op1=ALU.mult,
             )
-            nc.vector.tensor_tensor(out=cn8[:, m, :], in0=kept8[:, m, :], in1=added8[:, m, :], op=ALU.add)
+        for half in halves:
+            nc.vector.tensor_tensor(
+                out=cn8[:, half, :], in0=kept8[:, half, :], in1=added8[:, half, :], op=ALU.add
+            )
+        quantise(("o", 1))
+        for half in halves:
             nc.scalar.activation(
-                out=tanh_cn[:, m, :], in_=cn8[:, m, :], func=ACT.Tanh, scale=1.0 / NEW_SHARE
+                out=tanh_cn[:, half, :], in_=cn8[:, half, :], func=ACT.Tanh, scale=1.0 / NEW_SHARE
             )
-            nc.tensor.transpose(
-                out=c_natural[:, m * P : (m + 1) * P], in_=cn8[:, m, :], identity=ident_f32[:]
-            )
-        for m in range(TILES):
+        to_batch_major(c_natural, cn8, slice(0, TILES))
+        passes("o")
+        activations("o")
+
+        blend(c_sb, c_natural, out_1, slice(0, HID))
+        for half in halves:
             nc.vector.scalar_tensor_tensor(
-                out=hn8[:, m, :], in0=gate_act["o"][:, m, :], scalar=NEW_SHARE, in1=tanh_cn[:, m, :],
+                out=hn8[:, half, :], in0=gate_act["o"][:, half, :], scalar=NEW_SHARE, in1=tanh_cn[:, half, :],
                 op0=ALU.mult, op1=ALU.mult,
             )
-            nc.tensor.transpose(
-                out=h_natural[:, m * P : (m + 1) * P], in_=hn8[:, m, :], identity=ident_f32[:]
-            )
-
-        for old, new8, out in ((c_sb, c_natural, out_1), (h_sb, h_natural, out_0)):
-            result = const.tile([P, HID], F32, bufs=2)
-            nc.vector.scalar_tensor_tensor(
-                out=result[:], in0=old[:], scalar=OLD_SHARE, in1=new8[:], op0=ALU.mult, op1=ALU.add
-            )
-            nc.sync.dma_start(out=out, in_=result[:])
+            to_batch_major(h_natural, hn8, half)
+        blend(h_sb, h_natural, out_0, slice(0, HID))

@@ -21,7 +21,7 @@ GATE_FUNC = {"f": ACT.Sigmoid, "i": ACT.Sigmoid, "o": ACT.Sigmoid, "g": ACT.Tanh
 NEW_SHARE = 1.0 - 0.2
 OLD_SHARE = 1.0 - NEW_SHARE
 RUN = 4
-VECTOR_COLS = 272
+VECTOR_COLS = 296
 
 FLOPS = 2 * P * (2 * HID) * (len(GATE_ORDER) * HID)
 
@@ -44,6 +44,10 @@ def tile_lstmcell_pb_s_kernel(tc, x, h, c, mem_read, W_ih, W_hh, bias, out_0, ou
         make_identity(nc, ident_bf16[:])
         bias_rows = const.tile([P, P], BF16)
         nc.vector.memset(bias_rows[:], 0.0)
+        ident_quarter = const.tile([P, P], BF16)
+        nc.vector.tensor_scalar(
+            out=ident_quarter[:], in0=ident_bf16[:], scalar1=OLD_SHARE / NEW_SHARE, scalar2=None, op0=ALU.mult
+        )
 
         nc.scalar.dma_start(
             out=bias_rows[0 : len(GATE_ORDER) * TILES, :], in_=bias.rearrange("(r q) -> r q", q=P)
@@ -126,7 +130,7 @@ def tile_lstmcell_pb_s_kernel(tc, x, h, c, mem_read, W_ih, W_hh, bias, out_0, ou
         quantise(("i", 0))
         regroup(("i", 1))
 
-        xh_words = psum.tile([P, 2, 2, P], F32)
+        xh_words = psum.tile([P, 2, 2, P], F32, tag="xh_or_o")
         for s, rows in enumerate((x_sb, h_sb)):
             words = rows[:].bitcast(F32).rearrange("b (p u) -> b u p", u=2)
             for u in range(2):
@@ -136,40 +140,26 @@ def tile_lstmcell_pb_s_kernel(tc, x, h, c, mem_read, W_ih, W_hh, bias, out_0, ou
         xh_codes = const.tile([P, 2 * P], U32, align_bytes=64)
         xh_scales = const.tile([P, 2 * P], U8, align_bytes=64)
 
-        bias_ps = psum.tile([P, P], BF16, tag="c_natural")
+        bias_ps = psum.tile([P, P], BF16, tag="cn")
         nc.tensor.transpose(out=bias_ps[:], in_=bias_rows[:], identity=ident_bf16[:])
         bias_col = const.tile([P, len(GATE_ORDER) * TILES], F32)
         nc.scalar.copy(out=bias_col[:], in_=bias_ps[:, 0 : len(GATE_ORDER) * TILES])
-        cm_T = psum.tile([P, 2, TILES, P], BF16)
 
-        def to_hidden_major(which, rows):
+        fresh = const.tile([P, TILES, P], F32)
+        kept = const.tile([P, TILES, P], F32)
+        tanh_cn = const.tile([P, HID], F32)
+        hn8 = const.tile([P, HID], F32)
+        cn = psum.tile([P, HID], F32, tag="cn")
+        cn_c = psum.tile([P, HID], F32)
+        o_back = psum.tile([P, HID], F32, tag="xh_or_o")
+        c_T = psum.tile([P, TILES, P], BF16)
+
+        def add_transposed(bank, rows, stop=False):
             for m in range(TILES):
-                nc.tensor.transpose(
-                    out=cm_T[:, which, m, :], in_=rows[:, m * P : (m + 1) * P], identity=ident_bf16[:]
+                nc.tensor.matmul(
+                    out=bank[:, m * P : (m + 1) * P], lhsT=rows[:, m, :], rhs=ident_f32[:],
+                    is_transpose=True, start=False, stop=stop and m == TILES - 1,
                 )
-
-        fresh8 = const.tile([P, TILES, P], F32)
-        added8 = const.tile([P, TILES, P], F32)
-        kept8 = const.tile([P, TILES, P], F32)
-        cn8 = const.tile([P, TILES, P], F32)
-        tanh_cn = const.tile([P, TILES, P], F32)
-        hn8 = const.tile([P, TILES, P], F32)
-
-        c_natural = psum.tile([P, HID], F32, tag="c_natural")
-        h_natural = psum.tile([P, HID], F32)
-
-        def to_batch_major(natural, rows, half):
-            for m in range(half.start, half.stop):
-                nc.tensor.transpose(
-                    out=natural[:, m * P : (m + 1) * P], in_=rows[:, m, :], identity=ident_f32[:]
-                )
-
-        def blend(old, new8, out, cols):
-            result = const.tile([P, cols.stop - cols.start], F32, name="result", bufs=3)
-            nc.vector.scalar_tensor_tensor(
-                out=result[:], in0=old[:, cols], scalar=OLD_SHARE, in1=new8[:, cols], op0=ALU.mult, op1=ALU.add
-            )
-            nc.sync.dma_start(out=out[:, cols], in_=result[:])
 
         regroup(("g", 0))
         quantise(("i", 1))
@@ -185,48 +175,46 @@ def tile_lstmcell_pb_s_kernel(tc, x, h, c, mem_read, W_ih, W_hh, bias, out_0, ou
         regroup(("f", 0))
         quantise(("g", 1))
         passes("g")
-        to_hidden_major(1, mem_sb)
         regroup(("f", 1))
         quantise(("f", 0))
         activations("g")
-        regroup(("o", 0))
         quantise(("f", 1))
+        for m in range(TILES):
+            nc.tensor.transpose(out=c_T[:, m, :], in_=c_sb[:, m * P : (m + 1) * P], identity=ident_bf16[:])
         passes("f")
-        to_hidden_major(0, c_sb)
-        regroup(("o", 1))
-        activations("f")
-        nc.vector.scalar_tensor_tensor(
-            out=fresh8[:], in0=gate_act["i"][:], scalar=NEW_SHARE, in1=gate_act["g"][:],
-            op0=ALU.mult, op1=ALU.mult,
-        )
+        regroup(("o", 0))
+        nc.vector.tensor_tensor(out=fresh[:], in0=gate_act["i"][:], in1=gate_act["g"][:], op=ALU.mult)
         quantise(("o", 0))
-        nc.vector.scalar_tensor_tensor(
-            out=added8[:], in0=cm_T[:, 1], scalar=NEW_SHARE, in1=fresh8[:], op0=ALU.mult, op1=ALU.add
-        )
-        halves = [slice(0, TILES // 2), slice(TILES // 2, TILES)]
-        for half in halves:
-            nc.vector.scalar_tensor_tensor(
-                out=kept8[:, half, :], in0=gate_act["f"][:, half, :], scalar=NEW_SHARE, in1=cm_T[:, 0, half, :],
-                op0=ALU.mult, op1=ALU.mult,
-            )
-        for half in halves:
-            nc.vector.tensor_tensor(
-                out=cn8[:, half, :], in0=kept8[:, half, :], in1=added8[:, half, :], op=ALU.add
-            )
+        activations("f")
+        for bank in (cn, cn_c):
+            nc.tensor.matmul(out=bank[:], lhsT=ident_bf16[:], rhs=mem_sb[:], start=True, stop=False)
+        nc.tensor.matmul(out=cn_c[:], lhsT=ident_quarter[:], rhs=c_sb[:], start=False, stop=False)
+        add_transposed(cn, fresh)
+        add_transposed(cn_c, fresh)
+        nc.vector.tensor_tensor(out=kept[:], in0=gate_act["f"][:], in1=c_T[:], op=ALU.mult)
+        regroup(("o", 1))
+        add_transposed(cn, kept, stop=True)
+        nc.scalar.activation(out=tanh_cn[:], in_=cn[:], func=ACT.Tanh)
         quantise(("o", 1))
-        for half in halves:
-            nc.scalar.activation(
-                out=tanh_cn[:, half, :], in_=cn8[:, half, :], func=ACT.Tanh, scale=1.0 / NEW_SHARE
-            )
-        to_batch_major(c_natural, cn8, slice(0, TILES))
         passes("o")
+        add_transposed(cn_c, kept, stop=True)
         activations("o")
+        for m in range(TILES):
+            nc.tensor.transpose(
+                out=o_back[:, m * P : (m + 1) * P], in_=gate_act["o"][:, m, :], identity=ident_f32[:]
+            )
+        c_next = const.tile([P, HID], F32)
+        nc.scalar.activation(out=c_next[:], in_=cn_c[:], func=ACT.Copy, scale=NEW_SHARE)
+        nc.sync.dma_start(out=out_1, in_=c_next[:])
 
-        blend(c_sb, c_natural, out_1, slice(0, HID))
-        for half in halves:
+        for tiles in (range(0, TILES // 2), range(TILES // 2, TILES)):
+            cols = slice(tiles.start * P, tiles.stop * P)
             nc.vector.scalar_tensor_tensor(
-                out=hn8[:, half, :], in0=gate_act["o"][:, half, :], scalar=NEW_SHARE, in1=tanh_cn[:, half, :],
+                out=hn8[:, cols], in0=o_back[:, cols], scalar=NEW_SHARE, in1=tanh_cn[:, cols],
                 op0=ALU.mult, op1=ALU.mult,
             )
-            to_batch_major(h_natural, hn8, half)
-        blend(h_sb, h_natural, out_0, slice(0, HID))
+            h_next = const.tile([P, HID // 2], F32, bufs=2)
+            nc.vector.scalar_tensor_tensor(
+                out=h_next[:], in0=h_sb[:, cols], scalar=OLD_SHARE, in1=hn8[:, cols], op0=ALU.mult, op1=ALU.add
+            )
+            nc.sync.dma_start(out=out_0[:, cols], in_=h_next[:])

@@ -21,7 +21,7 @@ GATE_FUNC = {"f": ACT.Sigmoid, "i": ACT.Sigmoid, "o": ACT.Sigmoid, "g": ACT.Tanh
 NEW_SHARE = 1.0 - 0.2
 OLD_SHARE = 1.0 - NEW_SHARE
 RUN = 4
-VECTOR_COLS = 296
+VECTOR_COLS = 256
 
 FLOPS = 2 * P * (2 * HID) * (len(GATE_ORDER) * HID)
 
@@ -44,10 +44,6 @@ def tile_lstmcell_pb_s_kernel(tc, x, h, c, mem_read, W_ih, W_hh, bias, out_0, ou
         make_identity(nc, ident_bf16[:])
         bias_rows = const.tile([P, P], BF16)
         nc.vector.memset(bias_rows[:], 0.0)
-        ident_quarter = const.tile([P, P], BF16)
-        nc.vector.tensor_scalar(
-            out=ident_quarter[:], in0=ident_bf16[:], scalar1=OLD_SHARE / NEW_SHARE, scalar2=None, op0=ALU.mult
-        )
 
         nc.scalar.dma_start(
             out=bias_rows[0 : len(GATE_ORDER) * TILES, :], in_=bias.rearrange("(r q) -> r q", q=P)
@@ -71,7 +67,7 @@ def tile_lstmcell_pb_s_kernel(tc, x, h, c, mem_read, W_ih, W_hh, bias, out_0, ou
                 out=raw[key][:],
                 in_=(W_ih, W_hh)[s][:, block : block + HID].rearrange("(p t) n -> p t n", t=PACK),
             )
-            if key == units[1]:
+            if key == units[0]:
                 nc.sync.dma_start(out=x_sb[:], in_=x)
                 nc.sync.dma_start(out=h_sb[:], in_=h)
             if key == ("g", 1):
@@ -150,7 +146,7 @@ def tile_lstmcell_pb_s_kernel(tc, x, h, c, mem_read, W_ih, W_hh, bias, out_0, ou
         tanh_cn = const.tile([P, HID], F32)
         hn8 = const.tile([P, HID], F32)
         cn = psum.tile([P, HID], F32, tag="cn")
-        cn_c = psum.tile([P, HID], F32)
+        c_share = const.tile([P, HID], F32)
         o_back = psum.tile([P, HID], F32, tag="xh_or_o")
         c_T = psum.tile([P, TILES, P], BF16)
 
@@ -179,6 +175,7 @@ def tile_lstmcell_pb_s_kernel(tc, x, h, c, mem_read, W_ih, W_hh, bias, out_0, ou
         quantise(("f", 0))
         activations("g")
         quantise(("f", 1))
+        nc.vector.tensor_scalar(out=c_share[:], in0=c_sb[:], scalar1=OLD_SHARE, scalar2=None, op0=ALU.mult)
         for m in range(TILES):
             nc.tensor.transpose(out=c_T[:, m, :], in_=c_sb[:, m * P : (m + 1) * P], identity=ident_bf16[:])
         passes("f")
@@ -186,25 +183,23 @@ def tile_lstmcell_pb_s_kernel(tc, x, h, c, mem_read, W_ih, W_hh, bias, out_0, ou
         nc.vector.tensor_tensor(out=fresh[:], in0=gate_act["i"][:], in1=gate_act["g"][:], op=ALU.mult)
         quantise(("o", 0))
         activations("f")
-        for bank in (cn, cn_c):
-            nc.tensor.matmul(out=bank[:], lhsT=ident_bf16[:], rhs=mem_sb[:], start=True, stop=False)
-        nc.tensor.matmul(out=cn_c[:], lhsT=ident_quarter[:], rhs=c_sb[:], start=False, stop=False)
+        nc.tensor.matmul(out=cn[:], lhsT=ident_bf16[:], rhs=mem_sb[:], start=True, stop=False)
         add_transposed(cn, fresh)
-        add_transposed(cn_c, fresh)
         nc.vector.tensor_tensor(out=kept[:], in0=gate_act["f"][:], in1=c_T[:], op=ALU.mult)
         regroup(("o", 1))
         add_transposed(cn, kept, stop=True)
         nc.scalar.activation(out=tanh_cn[:], in_=cn[:], func=ACT.Tanh)
         quantise(("o", 1))
         passes("o")
-        add_transposed(cn_c, kept, stop=True)
         activations("o")
         for m in range(TILES):
             nc.tensor.transpose(
                 out=o_back[:, m * P : (m + 1) * P], in_=gate_act["o"][:, m, :], identity=ident_f32[:]
             )
         c_next = const.tile([P, HID], F32)
-        nc.scalar.activation(out=c_next[:], in_=cn_c[:], func=ACT.Copy, scale=NEW_SHARE)
+        nc.vector.scalar_tensor_tensor(
+            out=c_next[:], in0=cn[:], scalar=NEW_SHARE, in1=c_share[:], op0=ALU.mult, op1=ALU.add
+        )
         nc.sync.dma_start(out=out_1, in_=c_next[:])
 
         for tiles in (range(0, TILES // 2), range(TILES // 2, TILES)):

@@ -21,7 +21,7 @@ GATE_FUNC = {"f": ACT.Sigmoid, "i": ACT.Sigmoid, "o": ACT.Sigmoid, "g": ACT.Tanh
 NEW_SHARE = 1.0 - 0.2
 OLD_SHARE = 1.0 - NEW_SHARE
 RUN = 4
-VECTOR_COLS = 256
+VECTOR_COLS = 288
 
 FLOPS = 2 * P * (2 * HID) * (len(GATE_ORDER) * HID)
 
@@ -67,7 +67,7 @@ def tile_lstmcell_pb_s_kernel(tc, x, h, c, mem_read, W_ih, W_hh, bias, out_0, ou
                 out=raw[key][:],
                 in_=(W_ih, W_hh)[s][:, block : block + HID].rearrange("(p t) n -> p t n", t=PACK),
             )
-            if key == units[0]:
+            if key == units[1]:
                 nc.sync.dma_start(out=x_sb[:], in_=x)
                 nc.sync.dma_start(out=h_sb[:], in_=h)
             if key == ("g", 1):
@@ -78,7 +78,9 @@ def tile_lstmcell_pb_s_kernel(tc, x, h, c, mem_read, W_ih, W_hh, bias, out_0, ou
         gate_ps = {}
         gate_act = {}
         for gate in GATE_ORDER:
-            gate_ps[gate] = psum.tile([P, TILES, P], F32, name="bank_%s" % gate)
+            if gate != "o":
+                bank = psum.tile([P, TILES, P], F32, name="bank_%s" % gate, tag="bank_%s" % gate)
+                gate_ps[gate] = [bank[:, m, :] for m in range(TILES)]
             gate_act[gate] = const.tile([P, TILES, P], F32, name="act_%s" % gate)
 
         def regroup(key):
@@ -91,39 +93,41 @@ def tile_lstmcell_pb_s_kernel(tc, x, h, c, mem_read, W_ih, W_hh, bias, out_0, ou
                     in_=raw[key][:, :, cols].rearrange("p t (n i) -> p n t i", i=RUN),
                 )
 
-        def quantise(key):
+        def quantise(key, cols=slice(0, HID)):
             nc.vector.quantize_mx(
-                out=codes[key][:].bitcast(FP8X4),
-                scales=scales[key][:],
-                in_=grouped[key][:].rearrange("p n t -> p (n t)"),
+                out=codes[key][:, cols].bitcast(FP8X4),
+                scales=scales[key][:, cols],
+                in_=grouped[key][:, cols, :].rearrange("p n t -> p (n t)"),
+            )
+
+        def one_pass(gate, s, m):
+            cols = slice(m * P, (m + 1) * P)
+            nc.tensor.matmul_mx(
+                out=gate_ps[gate][m],
+                lhsT=codes[gate, s][:, cols].bitcast(FP8X4),
+                lhsT_scale=scales[gate, s][:, cols],
+                rhs=xh_codes[:, s * P : (s + 1) * P].bitcast(FP8X4),
+                rhs_scale=xh_scales[:, s * P : (s + 1) * P],
+                start=(s == 0),
+                stop=(s == 1),
             )
 
         def passes(gate):
             for m in range(TILES):
-                cols = slice(m * P, (m + 1) * P)
                 for s in range(2):
-                    nc.tensor.matmul_mx(
-                        out=gate_ps[gate][:, m, :],
-                        lhsT=codes[gate, s][:, cols].bitcast(FP8X4),
-                        lhsT_scale=scales[gate, s][:, cols],
-                        rhs=xh_codes[:, s * P : (s + 1) * P].bitcast(FP8X4),
-                        rhs_scale=xh_scales[:, s * P : (s + 1) * P],
-                        start=(s == 0),
-                        stop=(s == 1),
-                    )
+                    one_pass(gate, s, m)
 
         def activations(gate, tiles=range(TILES)):
             for m in tiles:
                 r = GATE_BLOCK[gate] * TILES + m
                 nc.scalar.activation(
                     out=gate_act[gate][:, m, :],
-                    in_=gate_ps[gate][:, m, :],
+                    in_=gate_ps[gate][m],
                     func=GATE_FUNC[gate],
                     bias=bias_col[:, r : r + 1],
                 )
 
         regroup(("i", 0))
-        quantise(("i", 0))
         regroup(("i", 1))
 
         xh_words = psum.tile([P, 2, 2, P], F32, tag="xh_or_o")
@@ -157,8 +161,9 @@ def tile_lstmcell_pb_s_kernel(tc, x, h, c, mem_read, W_ih, W_hh, bias, out_0, ou
                     is_transpose=True, start=False, stop=stop and m == TILES - 1,
                 )
 
-        regroup(("g", 0))
+        quantise(("i", 0))
         quantise(("i", 1))
+        regroup(("g", 0))
         nc.vector.quantize_mx(
             out=xh_codes[:].bitcast(FP8X4),
             scales=xh_scales[:],
@@ -168,29 +173,38 @@ def tile_lstmcell_pb_s_kernel(tc, x, h, c, mem_read, W_ih, W_hh, bias, out_0, ou
         regroup(("g", 1))
         quantise(("g", 0))
         activations("i")
-        regroup(("f", 0))
         quantise(("g", 1))
         passes("g")
+        regroup(("f", 0))
+        nc.tensor.matmul(out=cn[:], lhsT=ident_bf16[:], rhs=mem_sb[:], start=True, stop=False)
         regroup(("f", 1))
         quantise(("f", 0))
         activations("g")
         quantise(("f", 1))
-        nc.vector.tensor_scalar(out=c_share[:], in0=c_sb[:], scalar1=OLD_SHARE, scalar2=None, op0=ALU.mult)
         for m in range(TILES):
             nc.tensor.transpose(out=c_T[:, m, :], in_=c_sb[:, m * P : (m + 1) * P], identity=ident_bf16[:])
         passes("f")
         regroup(("o", 0))
+        nc.vector.tensor_scalar(out=c_share[:], in0=c_sb[:], scalar1=OLD_SHARE, scalar2=None, op0=ALU.mult)
         nc.vector.tensor_tensor(out=fresh[:], in0=gate_act["i"][:], in1=gate_act["g"][:], op=ALU.mult)
-        quantise(("o", 0))
-        activations("f")
-        nc.tensor.matmul(out=cn[:], lhsT=ident_bf16[:], rhs=mem_sb[:], start=True, stop=False)
         add_transposed(cn, fresh)
+        quantise(("o", 0))
+        gate_ps["o"] = []
+        for m, gate in enumerate(("i", "g", "o", "f")):
+            tile = psum.tile([P, P], F32, name="o_%d" % m, tag="bank_%s" % gate)
+            gate_ps["o"].append(tile[:])
+        for m in range(TILES - 1):
+            one_pass("o", 0, m)
+        activations("f")
+        one_pass("o", 0, TILES - 1)
         nc.vector.tensor_tensor(out=kept[:], in0=gate_act["f"][:], in1=c_T[:], op=ALU.mult)
         regroup(("o", 1))
         add_transposed(cn, kept, stop=True)
         nc.scalar.activation(out=tanh_cn[:], in_=cn[:], func=ACT.Tanh)
-        quantise(("o", 1))
-        passes("o")
+        quantise(("o", 1), slice(0, HID // 2))
+        quantise(("o", 1), slice(HID // 2, HID))
+        for m in range(TILES):
+            one_pass("o", 1, m)
         activations("o")
         for m in range(TILES):
             nc.tensor.transpose(
@@ -202,12 +216,13 @@ def tile_lstmcell_pb_s_kernel(tc, x, h, c, mem_read, W_ih, W_hh, bias, out_0, ou
         )
         nc.sync.dma_start(out=out_1, in_=c_next[:])
 
-        for tiles in (range(0, TILES // 2), range(TILES // 2, TILES)):
-            cols = slice(tiles.start * P, tiles.stop * P)
+        halves = [slice(0, HID // 2), slice(HID // 2, HID)]
+        for cols in halves:
             nc.vector.scalar_tensor_tensor(
                 out=hn8[:, cols], in0=o_back[:, cols], scalar=NEW_SHARE, in1=tanh_cn[:, cols],
                 op0=ALU.mult, op1=ALU.mult,
             )
+        for cols in halves:
             h_next = const.tile([P, HID // 2], F32, bufs=2)
             nc.vector.scalar_tensor_tensor(
                 out=h_next[:], in0=h_sb[:, cols], scalar=OLD_SHARE, in1=hn8[:, cols], op0=ALU.mult, op1=ALU.add

@@ -21,7 +21,7 @@ GATE_FUNC = {"f": ACT.Sigmoid, "i": ACT.Sigmoid, "o": ACT.Sigmoid, "g": ACT.Tanh
 NEW_SHARE = 1.0 - 0.2
 OLD_SHARE = 1.0 - NEW_SHARE
 RUN = 4
-VECTOR_COLS = 288
+VECTOR_COLS = 304
 
 FLOPS = 2 * P * (2 * HID) * (len(GATE_ORDER) * HID)
 
@@ -78,15 +78,21 @@ def tile_lstmcell_pb_s_kernel(tc, x, h, c, mem_read, W_ih, W_hh, bias, out_0, ou
         gate_ps = {}
         gate_act = {}
         for gate in GATE_ORDER:
-            if gate != "o":
-                bank = psum.tile([P, TILES, P], F32, name="bank_%s" % gate, tag="bank_%s" % gate)
-                gate_ps[gate] = [bank[:, m, :] for m in range(TILES)]
             gate_act[gate] = const.tile([P, TILES, P], F32, name="act_%s" % gate)
+        for j, gate in enumerate(("i", "g")):
+            bank = psum.tile([P, TILES, P], F32, name="ps_%s" % gate, tag="bank_%d" % j)
+            gate_ps[gate] = [bank[:, m, :] for m in range(TILES)]
 
-        def regroup(key):
+        def spread(gate, banks):
+            gate_ps[gate] = []
+            for m, j in enumerate(banks):
+                tile = psum.tile([P, P], F32, name="ps_%s%d" % (gate, m), tag="bank_%d" % j)
+                gate_ps[gate].append(tile[:])
+
+        def regroup(key, vector_cols=VECTOR_COLS):
             for copy, cols in (
-                (nc.vector.tensor_copy, slice(0, VECTOR_COLS)),
-                (nc.scalar.copy, slice(VECTOR_COLS, HID)),
+                (nc.vector.tensor_copy, slice(0, vector_cols)),
+                (nc.scalar.copy, slice(vector_cols, HID)),
             ):
                 copy(
                     out=grouped[key][:, cols, :].rearrange("p (n i) t -> p n t i", i=RUN),
@@ -163,12 +169,12 @@ def tile_lstmcell_pb_s_kernel(tc, x, h, c, mem_read, W_ih, W_hh, bias, out_0, ou
 
         quantise(("i", 0))
         quantise(("i", 1))
-        regroup(("g", 0))
         nc.vector.quantize_mx(
             out=xh_codes[:].bitcast(FP8X4),
             scales=xh_scales[:],
             in_=xh_grouped[:].rearrange("p s b t -> p (s b t)"),
         )
+        regroup(("g", 0))
         passes("i")
         regroup(("g", 1))
         quantise(("g", 0))
@@ -179,30 +185,31 @@ def tile_lstmcell_pb_s_kernel(tc, x, h, c, mem_read, W_ih, W_hh, bias, out_0, ou
         nc.tensor.matmul(out=cn[:], lhsT=ident_bf16[:], rhs=mem_sb[:], start=True, stop=False)
         regroup(("f", 1))
         quantise(("f", 0))
+        for m in range(TILES):
+            nc.tensor.transpose(out=c_T[:, m, :], in_=c_sb[:, m * P : (m + 1) * P], identity=ident_bf16[:])
+        spread("f", (2, 3, 4, 0))
+        for m in range(TILES):
+            one_pass("f", 0, m)
         activations("g")
         quantise(("f", 1))
         for m in range(TILES):
-            nc.tensor.transpose(out=c_T[:, m, :], in_=c_sb[:, m * P : (m + 1) * P], identity=ident_bf16[:])
-        passes("f")
-        regroup(("o", 0))
-        nc.vector.tensor_scalar(out=c_share[:], in0=c_sb[:], scalar1=OLD_SHARE, scalar2=None, op0=ALU.mult)
+            one_pass("f", 1, m)
+        regroup(("o", 0), 272)
         nc.vector.tensor_tensor(out=fresh[:], in0=gate_act["i"][:], in1=gate_act["g"][:], op=ALU.mult)
         add_transposed(cn, fresh)
         quantise(("o", 0))
-        gate_ps["o"] = []
-        for m, gate in enumerate(("i", "g", "o", "f")):
-            tile = psum.tile([P, P], F32, name="o_%d" % m, tag="bank_%s" % gate)
-            gate_ps["o"].append(tile[:])
-        for m in range(TILES - 1):
-            one_pass("o", 0, m)
+        spread("o", (1, 2, 3, 4))
+        one_pass("o", 0, 0)
         activations("f")
-        one_pass("o", 0, TILES - 1)
+        for m in range(1, TILES):
+            one_pass("o", 0, m)
         nc.vector.tensor_tensor(out=kept[:], in0=gate_act["f"][:], in1=c_T[:], op=ALU.mult)
-        regroup(("o", 1))
+        regroup(("o", 1), 272)
         add_transposed(cn, kept, stop=True)
         nc.scalar.activation(out=tanh_cn[:], in_=cn[:], func=ACT.Tanh)
         quantise(("o", 1), slice(0, HID // 2))
         quantise(("o", 1), slice(HID // 2, HID))
+        nc.vector.tensor_scalar(out=c_share[:], in0=c_sb[:], scalar1=OLD_SHARE, scalar2=None, op0=ALU.mult)
         for m in range(TILES):
             one_pass("o", 1, m)
         activations("o")

@@ -21,7 +21,7 @@ GATE_FUNC = {"f": ACT.Sigmoid, "i": ACT.Sigmoid, "o": ACT.Sigmoid, "g": ACT.Tanh
 NEW_SHARE = 1.0 - 0.2
 OLD_SHARE = 1.0 - NEW_SHARE
 RUN = 4
-VECTOR_COLS = 304
+VECTOR_COLS = 296
 
 FLOPS = 2 * P * (2 * HID) * (len(GATE_ORDER) * HID)
 
@@ -70,7 +70,7 @@ def tile_lstmcell_pb_s_kernel(tc, x, h, c, mem_read, W_ih, W_hh, bias, out_0, ou
             if key == units[1]:
                 nc.sync.dma_start(out=x_sb[:], in_=x)
                 nc.sync.dma_start(out=h_sb[:], in_=h)
-            if key == ("g", 1):
+            if key == ("o", 0):
                 nc.sync.dma_start(out=mem_sb[:], in_=mem_read)
             if key == ("f", 1):
                 nc.sync.dma_start(out=c_sb[:], in_=c)
@@ -89,14 +89,15 @@ def tile_lstmcell_pb_s_kernel(tc, x, h, c, mem_read, W_ih, W_hh, bias, out_0, ou
                 tile = psum.tile([P, P], F32, name="ps_%s%d" % (gate, m), tag="bank_%d" % j)
                 gate_ps[gate].append(tile[:])
 
-        def regroup(key, vector_cols=VECTOR_COLS):
-            for copy, cols in (
-                (nc.vector.tensor_copy, slice(0, vector_cols)),
-                (nc.scalar.copy, slice(vector_cols, HID)),
+        def regroup(key, vector_cols, cols=slice(0, HID)):
+            middle = cols.start + vector_cols
+            for copy, part in (
+                (nc.vector.tensor_copy, slice(cols.start, middle)),
+                (nc.scalar.copy, slice(middle, cols.stop)),
             ):
                 copy(
-                    out=grouped[key][:, cols, :].rearrange("p (n i) t -> p n t i", i=RUN),
-                    in_=raw[key][:, :, cols].rearrange("p t (n i) -> p n t i", i=RUN),
+                    out=grouped[key][:, part, :].rearrange("p (n i) t -> p n t i", i=RUN),
+                    in_=raw[key][:, :, part].rearrange("p t (n i) -> p n t i", i=RUN),
                 )
 
         def quantise(key, cols=slice(0, HID)):
@@ -133,8 +134,8 @@ def tile_lstmcell_pb_s_kernel(tc, x, h, c, mem_read, W_ih, W_hh, bias, out_0, ou
                     bias=bias_col[:, r : r + 1],
                 )
 
-        regroup(("i", 0))
-        regroup(("i", 1))
+        regroup(("i", 0), 288)
+        regroup(("i", 1), 288)
 
         xh_words = psum.tile([P, 2, 2, P], F32, tag="xh_or_o")
         for s, rows in enumerate((x_sb, h_sb)):
@@ -174,16 +175,15 @@ def tile_lstmcell_pb_s_kernel(tc, x, h, c, mem_read, W_ih, W_hh, bias, out_0, ou
             scales=xh_scales[:],
             in_=xh_grouped[:].rearrange("p s b t -> p (s b t)"),
         )
-        regroup(("g", 0))
+        regroup(("g", 0), 288)
         passes("i")
-        regroup(("g", 1))
+        regroup(("g", 1), 288)
         quantise(("g", 0))
         activations("i")
         quantise(("g", 1))
         passes("g")
-        regroup(("f", 0))
-        nc.tensor.matmul(out=cn[:], lhsT=ident_bf16[:], rhs=mem_sb[:], start=True, stop=False)
-        regroup(("f", 1))
+        regroup(("f", 0), 288)
+        regroup(("f", 1), 288)
         quantise(("f", 0))
         for m in range(TILES):
             nc.tensor.transpose(out=c_T[:, m, :], in_=c_sb[:, m * P : (m + 1) * P], identity=ident_bf16[:])
@@ -194,8 +194,9 @@ def tile_lstmcell_pb_s_kernel(tc, x, h, c, mem_read, W_ih, W_hh, bias, out_0, ou
         quantise(("f", 1))
         for m in range(TILES):
             one_pass("f", 1, m)
-        regroup(("o", 0), 272)
+        regroup(("o", 0), 288)
         nc.vector.tensor_tensor(out=fresh[:], in0=gate_act["i"][:], in1=gate_act["g"][:], op=ALU.mult)
+        nc.tensor.matmul(out=cn[:], lhsT=ident_bf16[:], rhs=mem_sb[:], start=True, stop=False)
         add_transposed(cn, fresh)
         quantise(("o", 0))
         spread("o", (1, 2, 3, 4))
@@ -204,7 +205,8 @@ def tile_lstmcell_pb_s_kernel(tc, x, h, c, mem_read, W_ih, W_hh, bias, out_0, ou
         for m in range(1, TILES):
             one_pass("o", 0, m)
         nc.vector.tensor_tensor(out=kept[:], in0=gate_act["f"][:], in1=c_T[:], op=ALU.mult)
-        regroup(("o", 1), 272)
+        for cols in (slice(0, HID // 2), slice(HID // 2, HID)):
+            regroup(("o", 1), 112, cols)
         add_transposed(cn, kept, stop=True)
         nc.scalar.activation(out=tanh_cn[:], in_=cn[:], func=ACT.Tanh)
         quantise(("o", 1), slice(0, HID // 2))

@@ -20,7 +20,7 @@ GATE_ORDER = ("i", "g", "f", "o")
 GATE_FUNC = {"f": ACT.Sigmoid, "i": ACT.Sigmoid, "o": ACT.Sigmoid, "g": ACT.Tanh}
 NEW_SHARE = 1.0 - 0.2
 OLD_SHARE = 1.0 - NEW_SHARE
-RUN = 4
+RUN = 2
 VECTOR_COLS = 296
 
 FLOPS = 2 * P * (2 * HID) * (len(GATE_ORDER) * HID)

@@ -70,10 +70,10 @@ def tile_lstmcell_pb_s_kernel(tc, x, h, c, mem_read, W_ih, W_hh, bias, out_0, ou
             if key == units[1]:
                 nc.sync.dma_start(out=x_sb[:], in_=x)
                 nc.sync.dma_start(out=h_sb[:], in_=h)
-            if key == ("o", 0):
-                nc.sync.dma_start(out=mem_sb[:], in_=mem_read)
             if key == ("f", 1):
                 nc.sync.dma_start(out=c_sb[:], in_=c)
+
+        nc.sync.dma_start(out=mem_sb[:], in_=mem_read)
 
         gate_ps = {}
         gate_act = {}
@@ -202,12 +202,13 @@ def tile_lstmcell_pb_s_kernel(tc, x, h, c, mem_read, W_ih, W_hh, bias, out_0, ou
         spread("o", (1, 2, 3, 4))
         one_pass("o", 0, 0)
         activations("f")
-        for m in range(1, TILES):
+        for m in range(1, TILES - 1):
             one_pass("o", 0, m)
         nc.vector.tensor_tensor(out=kept[:], in0=gate_act["f"][:], in1=c_T[:], op=ALU.mult)
         for cols in (slice(0, HID // 2), slice(HID // 2, HID)):
             regroup(("o", 1), 112, cols)
         add_transposed(cn, kept, stop=True)
+        one_pass("o", 0, TILES - 1)
         nc.scalar.activation(out=tanh_cn[:], in_=cn[:], func=ACT.Tanh)
         quantise(("o", 1), slice(0, HID // 2))
         quantise(("o", 1), slice(HID // 2, HID))

from contextlib import ExitStack

import concourse.mybir as mybir
from concourse.masks import make_identity

F32 = mybir.dt.float32
BF16 = mybir.dt.bfloat16
U32 = mybir.dt.uint32
U8 = mybir.dt.uint8
FP8X4 = mybir.dt.float8_e4m3fn_x4
ACT = mybir.ActivationFunctionType
ALU = mybir.AluOpType

P = 128
PACK = 4
HID = 512
TILES = HID // P
GATE_BLOCK = {"f": 0, "i": 1, "o": 2, "g": 3}
GATE_ORDER = ("i", "g", "f", "o")
GATE_FUNC = {"f": ACT.Sigmoid, "i": ACT.Sigmoid, "o": ACT.Sigmoid, "g": ACT.Tanh}
NEW_SHARE = 1.0 - 0.2
OLD_SHARE = 1.0 - NEW_SHARE
RUN = 2
VECTOR_COLS = 296

FLOPS = 2 * P * (2 * HID) * (len(GATE_ORDER) * HID)


def tile_lstmcell_pb_s_kernel(tc, x, h, c, mem_read, W_ih, W_hh, bias, out_0, out_1):
    nc = tc.nc
    units = [(gate, s) for gate in GATE_ORDER for s in range(2)]

    with ExitStack() as ctx:
        const = ctx.enter_context(tc.tile_pool(name="const", bufs=1))
        psum = ctx.enter_context(tc.psum_pool(name="psum", bufs=1))
        ctx.enter_context(tc.manual_schedule())

        warm = const.tile([P, 1], F32)
        nc.vector.memset(warm[:], 0.0)
        nc.scalar.activation(out=warm[:], in_=warm[:], func=ACT.Sigmoid)
        ident_f32 = const.tile([P, P], F32)
        make_identity(nc, ident_f32[:])
        ident_bf16 = const.tile([P, P], BF16)
        make_identity(nc, ident_bf16[:])
        bias_rows = const.tile([P, P], BF16)
        nc.vector.memset(bias_rows[:], 0.0)

        nc.scalar.dma_start(
            out=bias_rows[0 : len(GATE_ORDER) * TILES, :], in_=bias.rearrange("(r q) -> r q", q=P)
        )
        x_sb = const.tile([P, HID], BF16)
        h_sb = const.tile([P, HID], BF16)
        c_sb = const.tile([P, HID], BF16)
        mem_sb = const.tile([P, HID], BF16)
        raw = {}
        grouped = {}
        codes = {}
        scales = {}
        for key in units:
            gate, s = key
            raw[key] = const.tile([P, PACK, HID], BF16, name="raw_%s%d" % key)
            grouped[key] = const.tile([P, HID, PACK], BF16, name="grouped_%s%d" % key, align_bytes=64)
            codes[key] = const.tile([P, HID], U32, name="codes_%s%d" % key, align_bytes=64)
            scales[key] = const.tile([P, HID], U8, name="scales_%s%d" % key, align_bytes=64)
            block = GATE_BLOCK[gate] * HID
            nc.sync.dma_start(
                out=raw[key][:],
                in_=(W_ih, W_hh)[s][:, block : block + HID].rearrange("(p t) n -> p t n", t=PACK),
            )
            if key == units[1]:
                nc.sync.dma_start(out=x_sb[:], in_=x)
                nc.sync.dma_start(out=h_sb[:], in_=h)
            if key == ("f", 1):
                nc.sync.dma_start(out=c_sb[:], in_=c)

        nc.sync.dma_start(out=mem_sb[:], in_=mem_read)

        gate_ps = {}
        gate_act = {}
        for gate in GATE_ORDER:
            gate_act[gate] = const.tile([P, TILES, P], F32, name="act_%s" % gate)
        for j, gate in enumerate(("i", "g")):
            bank = psum.tile([P, TILES, P], F32, name="ps_%s" % gate, tag="bank_%d" % j)
            gate_ps[gate] = [bank[:, m, :] for m in range(TILES)]

        def spread(gate, banks):
            gate_ps[gate] = []
            for m, j in enumerate(banks):
                tile = psum.tile([P, P], F32, name="ps_%s%d" % (gate, m), tag="bank_%d" % j)
                gate_ps[gate].append(tile[:])

        def regroup(key, vector_cols, cols=slice(0, HID)):
            middle = cols.start + vector_cols
            for copy, part in (
                (nc.vector.tensor_copy, slice(cols.start, middle)),
                (nc.scalar.copy, slice(middle, cols.stop)),
            ):
                copy(
                    out=grouped[key][:, part, :].rearrange("p (n i) t -> p n t i", i=RUN),
                    in_=raw[key][:, :, part].rearrange("p t (n i) -> p n t i", i=RUN),
                )

        def quantise(key, cols=slice(0, HID)):
            nc.vector.quantize_mx(
                out=codes[key][:, cols].bitcast(FP8X4),
                scales=scales[key][:, cols],
                in_=grouped[key][:, cols, :].rearrange("p n t -> p (n t)"),
            )

        def one_pass(gate, s, m):
            cols = slice(m * P, (m + 1) * P)
            nc.tensor.matmul_mx(
                out=gate_ps[gate][m],
                lhsT=codes[gate, s][:, cols].bitcast(FP8X4),
                lhsT_scale=scales[gate, s][:, cols],
                rhs=xh_codes[:, s * P : (s + 1) * P].bitcast(FP8X4),
                rhs_scale=xh_scales[:, s * P : (s + 1) * P],
                start=(s == 0),
                stop=(s == 1),
            )

        def passes(gate):
            for m in range(TILES):
                for s in range(2):
                    one_pass(gate, s, m)

        def activations(gate, tiles=range(TILES)):
            for m in tiles:
                r = GATE_BLOCK[gate] * TILES + m
                nc.scalar.activation(
                    out=gate_act[gate][:, m, :],
                    in_=gate_ps[gate][m],
                    func=GATE_FUNC[gate],
                    bias=bias_col[:, r : r + 1],
                )

        regroup(("i", 0), 288)
        regroup(("i", 1), 288)

        xh_words = psum.tile([P, 2, 2, P], F32, tag="xh_or_o")
        for s, rows in enumerate((x_sb, h_sb)):
            words = rows[:].bitcast(F32).rearrange("b (p u) -> b u p", u=2)
            for u in range(2):
                nc.tensor.transpose(out=xh_words[:, s, u, :], in_=words[:, u, :], identity=ident_f32[:])
        xh_grouped = const.tile([P, 2, P, PACK], BF16, align_bytes=64)
        nc.scalar.copy(out=xh_grouped[:].bitcast(F32), in_=xh_words[:].rearrange("p s u b -> p s b u"))
        xh_codes = const.tile([P, 2 * P], U32, align_bytes=64)
        xh_scales = const.tile([P, 2 * P], U8, align_bytes=64)

        bias_ps = psum.tile([P, P], BF16, tag="cn")
        nc.tensor.transpose(out=bias_ps[:], in_=bias_rows[:], identity=ident_bf16[:])
        bias_col = const.tile([P, len(GATE_ORDER) * TILES], F32)
        nc.scalar.copy(out=bias_col[:], in_=bias_ps[:, 0 : len(GATE_ORDER) * TILES])

        fresh = const.tile([P, TILES, P], F32)
        kept = const.tile([P, TILES, P], F32)
        tanh_cn = const.tile([P, HID], F32)
        hn8 = const.tile([P, HID], F32)
        cn = psum.tile([P, HID], F32, tag="cn")
        c_share = const.tile([P, HID], F32)
        o_back = psum.tile([P, HID], F32, tag="xh_or_o")
        c_T = psum.tile([P, TILES, P], BF16)

        def add_transposed(bank, rows, stop=False):
            for m in range(TILES):
                nc.tensor.matmul(
                    out=bank[:, m * P : (m + 1) * P], lhsT=rows[:, m, :], rhs=ident_f32[:],
                    is_transpose=True, start=False, stop=stop and m == TILES - 1,
                )

        quantise(("i", 0))
        quantise(("i", 1))
        nc.vector.quantize_mx(
            out=xh_codes[:].bitcast(FP8X4),
            scales=xh_scales[:],
            in_=xh_grouped[:].rearrange("p s b t -> p (s b t)"),
        )
        regroup(("g", 0), 288)
        passes("i")
        regroup(("g", 1), 288)
        quantise(("g", 0))
        activations("i")
        quantise(("g", 1))
        passes("g")
        regroup(("f", 0), 288)
        regroup(("f", 1), 288)
        quantise(("f", 0))
        for m in range(TILES):
            nc.tensor.transpose(out=c_T[:, m, :], in_=c_sb[:, m * P : (m + 1) * P], identity=ident_bf16[:])
        spread("f", (2, 3, 4, 0))
        for m in range(TILES):
            one_pass("f", 0, m)
        activations("g")
        quantise(("f", 1))
        for m in range(TILES):
            one_pass("f", 1, m)
        regroup(("o", 0), 288)
        nc.vector.tensor_tensor(out=fresh[:], in0=gate_act["i"][:], in1=gate_act["g"][:], op=ALU.mult)
        nc.tensor.matmul(out=cn[:], lhsT=ident_bf16[:], rhs=mem_sb[:], start=True, stop=False)
        add_transposed(cn, fresh)
        quantise(("o", 0))
        spread("o", (1, 2, 3, 4))
        one_pass("o", 0, 0)
        activations("f")
        for m in range(1, TILES - 1):
            one_pass("o", 0, m)
        nc.vector.tensor_tensor(out=kept[:], in0=gate_act["f"][:], in1=c_T[:], op=ALU.mult)
        for cols in (slice(0, HID // 2), slice(HID // 2, HID)):
            regroup(("o", 1), 112, cols)
        add_transposed(cn, kept, stop=True)
        one_pass("o", 0, TILES - 1)
        nc.scalar.activation(out=tanh_cn[:], in_=cn[:], func=ACT.Tanh)
        quantise(("o", 1), slice(0, HID // 2))
        quantise(("o", 1), slice(HID // 2, HID))
        nc.vector.tensor_scalar(out=c_share[:], in0=c_sb[:], scalar1=OLD_SHARE, scalar2=None, op0=ALU.mult)
        for m in range(TILES):
            one_pass("o", 1, m)
        activations("o")
        for m in range(TILES):
            nc.tensor.transpose(
                out=o_back[:, m * P : (m + 1) * P], in_=gate_act["o"][:, m, :], identity=ident_f32[:]
            )
        c_next = const.tile([P, HID], F32)
        nc.vector.scalar_tensor_tensor(
            out=c_next[:], in0=cn[:], scalar=NEW_SHARE, in1=c_share[:], op0=ALU.mult, op1=ALU.add
        )
        nc.sync.dma_start(out=out_1, in_=c_next[:])

        halves = [slice(0, HID // 2), slice(HID // 2, HID)]
        for cols in halves:
            nc.vector.scalar_tensor_tensor(
                out=hn8[:, cols], in0=o_back[:, cols], scalar=NEW_SHARE, in1=tanh_cn[:, cols],
                op0=ALU.mult, op1=ALU.mult,
            )
        for cols in halves:
            h_next = const.tile([P, HID // 2], F32, bufs=2)
            nc.vector.scalar_tensor_tensor(
                out=h_next[:], in0=h_sb[:, cols], scalar=OLD_SHARE, in1=hn8[:, cols], op0=ALU.mult, op1=ALU.add
            )
            nc.sync.dma_start(out=out_0[:, cols], in_=h_next[:])
